import numpy as np
import ml_dtypes


def mxq(x, axis, fmt="e4m3"):
    dtype, down = {"e4m3": (ml_dtypes.float8_e4m3fn, 7), "e5m2": (ml_dtypes.float8_e5m2, 14)}[fmt]
    v = np.moveaxis(np.asarray(x, np.float32).astype(ml_dtypes.bfloat16).astype(np.float64), axis, -1)
    blocks = v.reshape(v.shape[:-1] + (-1, 32))
    amax = np.abs(blocks).max(-1, keepdims=True)
    byte = np.maximum(np.where(amax > 0, np.frexp(amax)[1] - 1 + 127, 0) - down, 1)
    scale = np.exp2(byte - 127.0)
    codes = (blocks / scale).astype(np.float32).astype(dtype).astype(np.float64)
    return np.moveaxis((codes * scale).reshape(v.shape), -1, axis)


WIDE = False


def mx_kscale(k):
    if not WIDE:
        return np.ones(k)
    levels = np.array([20, -20, 10, -10, 0])
    a = np.random.permutation(np.resize(levels, k // 512 * 4)).reshape(k // 512, 4)
    idx = np.arange(k)
    return np.exp2(a[idx // 512, idx % 128 // 32])


BF16 = ml_dtypes.bfloat16


def bf(x):
    return np.asarray(x, np.float32).astype(BF16)


def f64(x):
    return np.asarray(x).astype(np.float64)


NP, NH, NF, NU, B, C, H, W, IN_DIM = 7, 3, 2, 4, 4, 512, 8, 16, 256
S = H * W
EPS = 1e-5
PARENT = [0, 1, 1, 1, 1, 2, 2]


def make_bn():
    return bf(np.stack([1.0 + 0.1 * np.random.standard_normal(C), 0.1 * np.random.standard_normal(C),
                        0.1 * np.random.standard_normal(C), np.random.uniform(0.5, 1.5, C)]))


def make_w():
    return bf(np.random.standard_normal((C, 2 * C)) / np.sqrt(2 * C))


def make_nodes(n):
    return bf(np.random.standard_normal((n, B, C, H, W)))


def bn_scale_shift(bn):
    gamma, beta, mean, var = f64(bn)
    scale = gamma / np.sqrt(var + EPS)
    return scale, beta - mean * scale


def pre_relu(p_nodes, h_nodes, W_decomp_half, bn_decomp_half, W_bg_p, bn_bg_p):
    p = f64(p_nodes).reshape(NP, B, C, S)
    h = f64(h_nodes).reshape(NH, B, C, S)
    zs = []
    for n in range(NP):
        wf, bn = (f64(W_bg_p), bn_bg_p) if n == 0 else (f64(W_decomp_half), bn_decomp_half)
        scale, shift = bn_scale_shift(bn)
        y = wf[:, :C] @ h[PARENT[n]] + wf[:, C:] @ p[n]
        zs.append(y * scale[:, None] + shift[:, None])
    return np.stack(zs).reshape(NP, B, C, H, W)


def setup_inputs():
    u = mx_kscale(C)
    p = make_nodes(NP)
    h = make_nodes(NH)
    wd0 = make_w()
    bnd = make_bn()
    wb0 = make_w()
    bnb = make_bn()
    g = bf(np.random.standard_normal((NP, B, C, H, W)) * np.exp2(np.random.randint(-12, 1, (NP, B, 1, H, W)))
           * 8.0 * u[:, None, None])
    z = pre_relu(p, h, wd0, bnd, wb0, bnb)
    return {'p_nodes': p, 'h_nodes': h,
            'W_decomp_half': bf(f64(wd0) / u[:, None]), 'bn_decomp_half': bnd,
            'W_bg_p': bf(f64(wb0) / u[:, None]), 'bn_bg_p': bnb,
            'z': np.asarray(z, np.float32), 'grad_out': g}


def reference(p_nodes, h_nodes, W_decomp_half, bn_decomp_half, W_bg_p, bn_bg_p, z, grad_out):
    g = f64(grad_out).reshape(NP, B, C, S)
    zf = f64(z).reshape(NP, B, C, S)
    sb = bn_scale_shift(bn_bg_p)[0]
    sd = bn_scale_shift(bn_decomp_half)[0]
    scale = np.stack([sb] + [sd] * (NP - 1))
    dz = np.where(zf > 0.0, g * scale[:, None, :, None], 0.0)
    d0 = mxq(dz[0].transpose(1, 0, 2).reshape(C, B * S), 0, 'e5m2')
    dd = mxq(dz[1:].transpose(2, 0, 1, 3).reshape(C, (NP - 1) * B * S), 0, 'e5m2')
    wb = mxq(f64(W_bg_p)[:, C:], 0, 'e4m3')
    wd = mxq(f64(W_decomp_half)[:, C:], 0, 'e4m3')
    o0 = (wb.T @ d0).reshape(C, 1, B, S)
    od = (wd.T @ dd).reshape(C, NP - 1, B, S)
    return np.concatenate([o0, od], axis=1).transpose(1, 2, 0, 3).reshape(NP, B, C, H, W)

@@ -1,0 +1,164 @@
+from contextlib import ExitStack
+
+import concourse.mybir as mybir
+
+F32 = mybir.dt.float32
+BF16 = mybir.dt.bfloat16
+U32 = mybir.dt.uint32
+U8 = mybir.dt.uint8
+E4M3_X4 = mybir.dt.float8_e4m3fn_x4
+E5M2_X4 = mybir.dt.float8_e5m2_x4
+ALU = mybir.AluOpType
+ACT = mybir.ActivationFunctionType
+
+P = 128
+PACK = 4
+NODES = 7
+BATCH = 4
+CH = 512
+POS = 128
+COLS = BATCH * POS
+OUT_TILES = CH // P
+EPS = 1e-5
+GAMMA_ROW = 0
+VAR_ROW = 3
+BN_ROWS = 4
+
+FLOPS = 2 * NODES * COLS * CH * CH
+BYTES = NODES * COLS * CH * (4 + 2 + 4) + 2 * CH * CH * 2 + 2 * BN_ROWS * CH * 2
+
+
+def tile_gnn_pb_v_kernel(
+    tc, p_nodes, h_nodes, W_decomp_half, bn_decomp_half, W_bg_p, bn_bg_p, z, grad_out, out
+):
+    nc = tc.nc
+    weights = [W_bg_p, W_decomp_half]
+    norms = [bn_bg_p, bn_decomp_half]
+    kinds = len(weights)
+
+    with ExitStack() as ctx:
+        consts = ctx.enter_context(tc.tile_pool(name="consts", bufs=1))
+        wpool = ctx.enter_context(tc.tile_pool(name="wpool", bufs=kinds))
+        loads = ctx.enter_context(tc.tile_pool(name="loads", bufs=NODES))
+        work = ctx.enter_context(tc.tile_pool(name="work", bufs=3))
+        results = ctx.enter_context(tc.tile_pool(name="results", bufs=NODES))
+        psum = ctx.enter_context(tc.psum_pool(name="psum", bufs=2 * OUT_TILES))
+
+        bn_sb = consts.tile([P, kinds, BN_ROWS, PACK], BF16)
+        for kind in range(kinds):
+            nc.scalar.dma_start(
+                out=bn_sb[:, kind], in_=norms[kind].rearrange("r (p t) -> p r t", t=PACK)
+            )
+
+        w_raws = []
+        g_tiles = []
+        z_tiles = []
+        for n in range(NODES):
+            if n < kinds:
+                w_raw = wpool.tile([P, PACK, CH], BF16)
+                nc.sync.dma_start(
+                    out=w_raw[:],
+                    in_=weights[n][:, CH : 2 * CH].rearrange("(p t) c -> p t c", t=PACK),
+                )
+                w_raws.append(w_raw)
+            g_sb = loads.tile([P, BATCH, PACK, POS], BF16)
+            nc.sync.dma_start(
+                out=g_sb[:].rearrange("p b t s -> p b (t s)"),
+                in_=grad_out[n].rearrange("b (p t) i j -> p b (t i j)", t=PACK),
+            )
+            g_tiles.append(g_sb)
+            z_sb = loads.tile([P, BATCH, PACK, POS], F32)
+            nc.sync.dma_start(
+                out=z_sb[:].rearrange("p b t s -> p b (t s)"),
+                in_=z[n].rearrange("b (p t) i j -> p b (t i j)", t=PACK),
+            )
+            z_tiles.append(z_sb)
+
+        var_eps = consts.tile([P, kinds, PACK], F32)
+        nc.vector.tensor_scalar_add(out=var_eps[:], in0=bn_sb[:, :, VAR_ROW, :], scalar1=EPS)
+        std = consts.tile([P, kinds, PACK], F32)
+        nc.scalar.sqrt(out=std[:], in_=var_eps[:])
+        inv_std = consts.tile([P, kinds, PACK], F32)
+        nc.vector.reciprocal(out=inv_std[:], in_=std[:])
+        bn_scale = consts.tile([P, kinds, PACK], F32)
+        nc.vector.tensor_mul(out=bn_scale[:], in0=inv_std[:], in1=bn_sb[:, :, GAMMA_ROW, :])
+
+        w_codes_tiles = []
+        w_scales_tiles = []
+        for kind in range(kinds):
+            w_grouped = wpool.tile([P, OUT_TILES, P, PACK], BF16, align_bytes=64)
+            nc.vector.tensor_copy(
+                out=w_grouped[:],
+                in_=w_raws[kind][:].rearrange("p t (q m) -> p m q t", m=OUT_TILES),
+            )
+            w_codes = wpool.tile([P, CH], U32, align_bytes=64)
+            w_scales = wpool.tile([P, CH], U8, align_bytes=64)
+            nc.vector.quantize_mx(
+                out=w_codes[:].bitcast(E4M3_X4),
+                scales=w_scales[:],
+                in_=w_grouped[:].rearrange("p m q t -> p (m q t)"),
+            )
+            w_codes_tiles.append(w_codes)
+            w_scales_tiles.append(w_scales)
+
+        def quantise_dz(n):
+            kind = min(n, 1)
+            scaled = work.tile([P, BATCH, PACK, POS], BF16)
+            for t in range(PACK):
+                nc.scalar.activation(
+                    out=scaled[:, :, t, :],
+                    in_=g_tiles[n][:, :, t, :],
+                    func=ACT.Copy,
+                    scale=bn_scale[:, kind, t : t + 1],
+                )
+            dz = work.tile([P, BATCH, POS, PACK], BF16, align_bytes=64)
+            for b in range(BATCH):
+                nc.vector.scalar_tensor_tensor(
+                    out=dz[:, b],
+                    in0=z_tiles[n][:, b].rearrange("p t s -> p s t"),
+                    scalar=0.0,
+                    in1=scaled[:, b].rearrange("p t s -> p s t"),
+                    op0=ALU.is_gt,
+                    op1=ALU.mult,
+                )
+            dz_codes = work.tile([P, COLS], U32, align_bytes=64)
+            dz_scales = work.tile([P, COLS], U8, align_bytes=64)
+            nc.vector.quantize_mx(
+                out=dz_codes[:].bitcast(E5M2_X4),
+                scales=dz_scales[:],
+                in_=dz[:].rearrange("p b s t -> p (b s t)"),
+            )
+            return dz_codes, dz_scales
+
+        def multiply_and_store(n, dz_codes, dz_scales):
+            kind = min(n, 1)
+            res = results.tile([P, BATCH, OUT_TILES, POS], F32)
+            for m in range(OUT_TILES):
+                m_cols = slice(m * P, (m + 1) * P)
+                acc = psum.tile([P, COLS], F32)
+                nc.tensor.matmul_mx(
+                    out=acc[:],
+                    lhsT=w_codes_tiles[kind][:, m_cols].bitcast(E4M3_X4),
+                    lhsT_scale=w_scales_tiles[kind][:, m_cols],
+                    rhs=dz_codes[:].bitcast(E5M2_X4),
+                    rhs_scale=dz_scales[:],
+                    start=True,
+                    stop=True,
+                )
+                acc_view = acc[:].rearrange("p (b s) -> p b s", b=BATCH)
+                if m % 2 == 0:
+                    nc.scalar.copy(out=res[:, :, m, :], in_=acc_view)
+                else:
+                    nc.vector.tensor_copy(out=res[:, :, m, :], in_=acc_view)
+            nc.sync.dma_start(
+                out=out[n].rearrange("b (q m) i j -> q b (m i j)", m=OUT_TILES),
+                in_=res[:].rearrange("q b m s -> q b (m s)"),
+            )
+
+        previous = None
+        for n in range(NODES):
+            current = quantise_dz(n)
+            if previous is not None:
+                multiply_and_store(n - 1, previous[0], previous[1])
+            previous = current
+        multiply_and_store(NODES - 1, previous[0], previous[1])

@@ -9,7 +9,6 @@ U8 = mybir.dt.uint8
 E4M3_X4 = mybir.dt.float8_e4m3fn_x4
 E5M2_X4 = mybir.dt.float8_e5m2_x4
 ALU = mybir.AluOpType
-ACT = mybir.ActivationFunctionType
 
 P = 128
 PACK = 4
@@ -20,12 +19,15 @@ POS = 128
 COLS = BATCH * POS
 OUT_TILES = CH // P
 EPS = 1e-5
+BN_ROWS = 4
 GAMMA_ROW = 0
 VAR_ROW = 3
-BN_ROWS = 4
+BN_SLOTS = 4
+GAMMA_SLOT = 0
+VAR_SLOT = 1
 
 FLOPS = 2 * NODES * COLS * CH * CH
-BYTES = NODES * COLS * CH * (4 + 2 + 4) + 2 * CH * CH * 2 + 2 * BN_ROWS * CH * 2
+BYTES = NODES * COLS * CH * (4 + 2 + 4) + 2 * CH * CH * 2 + 2 * 2 * CH * 2
 
 
 def tile_gnn_pb_v_kernel(
@@ -43,11 +45,14 @@ def tile_gnn_pb_v_kernel(
         work = ctx.enter_context(tc.tile_pool(name="work", bufs=3))
         results = ctx.enter_context(tc.tile_pool(name="results", bufs=NODES))
         psum = ctx.enter_context(tc.psum_pool(name="psum", bufs=2 * OUT_TILES))
+        ctx.enter_context(tc.manual_schedule())
 
-        bn_sb = consts.tile([P, kinds, BN_ROWS, PACK], BF16)
+        bn_sb = consts.tile([P, kinds, BN_SLOTS, PACK], BF16)
         for kind in range(kinds):
+            table = norms[kind].rearrange("r (p t) -> p r t", t=PACK)
             nc.scalar.dma_start(
-                out=bn_sb[:, kind], in_=norms[kind].rearrange("r (p t) -> p r t", t=PACK)
+                out=bn_sb[:, kind, GAMMA_SLOT : VAR_SLOT + 1, :],
+                in_=table[:, GAMMA_ROW : BN_ROWS : VAR_ROW - GAMMA_ROW, :],
             )
 
         w_raws = []
@@ -75,41 +80,45 @@ def tile_gnn_pb_v_kernel(
             z_tiles.append(z_sb)
 
         var_eps = consts.tile([P, kinds, PACK], F32)
-        nc.vector.tensor_scalar_add(out=var_eps[:], in0=bn_sb[:, :, VAR_ROW, :], scalar1=EPS)
+        nc.vector.tensor_scalar_add(out=var_eps[:], in0=bn_sb[:, :, VAR_SLOT, :], scalar1=EPS)
         std = consts.tile([P, kinds, PACK], F32)
         nc.scalar.sqrt(out=std[:], in_=var_eps[:])
         inv_std = consts.tile([P, kinds, PACK], F32)
         nc.vector.reciprocal(out=inv_std[:], in_=std[:])
         bn_scale = consts.tile([P, kinds, PACK], F32)
-        nc.vector.tensor_mul(out=bn_scale[:], in0=inv_std[:], in1=bn_sb[:, :, GAMMA_ROW, :])
+        nc.vector.tensor_mul(out=bn_scale[:], in0=inv_std[:], in1=bn_sb[:, :, GAMMA_SLOT, :])
 
-        w_codes_tiles = []
-        w_scales_tiles = []
+        w_grouped_tiles = []
         for kind in range(kinds):
             w_grouped = wpool.tile([P, OUT_TILES, P, PACK], BF16, align_bytes=64)
-            nc.vector.tensor_copy(
+            nc.scalar.copy(
                 out=w_grouped[:],
                 in_=w_raws[kind][:].rearrange("p t (q m) -> p m q t", m=OUT_TILES),
             )
-            w_codes = wpool.tile([P, CH], U32, align_bytes=64)
-            w_scales = wpool.tile([P, CH], U8, align_bytes=64)
-            nc.vector.quantize_mx(
-                out=w_codes[:].bitcast(E4M3_X4),
-                scales=w_scales[:],
-                in_=w_grouped[:].rearrange("p m q t -> p (m q t)"),
-            )
-            w_codes_tiles.append(w_codes)
-            w_scales_tiles.append(w_scales)
+            w_grouped_tiles.append(w_grouped)
 
-        def quantise_dz(n):
-            kind = min(n, 1)
+        w_codes_tiles = []
+        w_scales_tiles = []
+        for n in range(NODES):
+            kind = min(n, kinds - 1)
+
+            if n < kinds:
+                w_codes = wpool.tile([P, CH], U32, align_bytes=64)
+                w_scales = wpool.tile([P, CH], U8, align_bytes=64)
+                nc.vector.quantize_mx(
+                    out=w_codes[:].bitcast(E4M3_X4),
+                    scales=w_scales[:],
+                    in_=w_grouped_tiles[n][:].rearrange("p m q t -> p (m q t)"),
+                )
+                w_codes_tiles.append(w_codes)
+                w_scales_tiles.append(w_scales)
+
             scaled = work.tile([P, BATCH, PACK, POS], BF16)
             for t in range(PACK):
-                nc.scalar.activation(
+                nc.vector.tensor_scalar_mul(
                     out=scaled[:, :, t, :],
-                    in_=g_tiles[n][:, :, t, :],
-                    func=ACT.Copy,
-                    scale=bn_scale[:, kind, t : t + 1],
+                    in0=g_tiles[n][:, :, t, :],
+                    scalar1=bn_scale[:, kind, t : t + 1],
                 )
             dz = work.tile([P, BATCH, POS, PACK], BF16, align_bytes=64)
             for b in range(BATCH):
@@ -128,10 +137,7 @@ def tile_gnn_pb_v_kernel(
                 scales=dz_scales[:],
                 in_=dz[:].rearrange("p b s t -> p (b s t)"),
             )
-            return dz_codes, dz_scales
 
-        def multiply_and_store(n, dz_codes, dz_scales):
-            kind = min(n, 1)
             res = results.tile([P, BATCH, OUT_TILES, POS], F32)
             for m in range(OUT_TILES):
                 m_cols = slice(m * P, (m + 1) * P)
@@ -145,20 +151,10 @@ def tile_gnn_pb_v_kernel(
                     start=True,
                     stop=True,
                 )
-                acc_view = acc[:].rearrange("p (b s) -> p b s", b=BATCH)
-                if m % 2 == 0:
-                    nc.scalar.copy(out=res[:, :, m, :], in_=acc_view)
-                else:
-                    nc.vector.tensor_copy(out=res[:, :, m, :], in_=acc_view)
+                nc.scalar.copy(
+                    out=res[:, :, m, :], in_=acc[:].rearrange("p (b s) -> p b s", b=BATCH)
+                )
             nc.sync.dma_start(
                 out=out[n].rearrange("b (q m) i j -> q b (m i j)", m=OUT_TILES),
                 in_=res[:].rearrange("q b m s -> q b (m s)"),
             )
-
-        previous = None
-        for n in range(NODES):
-            current = quantise_dz(n)
-            if previous is not None:
-                multiply_and_store(n - 1, previous[0], previous[1])
-            previous = current
-        multiply_and_store(NODES - 1, previous[0], previous[1])

@@ -25,6 +25,7 @@ VAR_ROW = 3
 BN_SLOTS = 4
 GAMMA_SLOT = 0
 VAR_SLOT = 1
+SCALAR_BATCHES = 3
 
 FLOPS = 2 * NODES * COLS * CH * CH
 BYTES = NODES * COLS * CH * (4 + 2 + 4) + 2 * CH * CH * 2 + 2 * 2 * CH * 2
@@ -99,20 +100,20 @@ def tile_gnn_pb_v_kernel(
 
         w_codes_tiles = []
         w_scales_tiles = []
-        for n in range(NODES):
+
+        def quantize_weight(kind):
+            w_codes = wpool.tile([P, CH], U32, align_bytes=64)
+            w_scales = wpool.tile([P, CH], U8, align_bytes=64)
+            nc.vector.quantize_mx(
+                out=w_codes[:].bitcast(E4M3_X4),
+                scales=w_scales[:],
+                in_=w_grouped_tiles[kind][:].rearrange("p m q t -> p (m q t)"),
+            )
+            w_codes_tiles.append(w_codes)
+            w_scales_tiles.append(w_scales)
+
+        def scale_node(n):
             kind = min(n, kinds - 1)
-
-            if n < kinds:
-                w_codes = wpool.tile([P, CH], U32, align_bytes=64)
-                w_scales = wpool.tile([P, CH], U8, align_bytes=64)
-                nc.vector.quantize_mx(
-                    out=w_codes[:].bitcast(E4M3_X4),
-                    scales=w_scales[:],
-                    in_=w_grouped_tiles[n][:].rearrange("p m q t -> p (m q t)"),
-                )
-                w_codes_tiles.append(w_codes)
-                w_scales_tiles.append(w_scales)
-
             scaled = work.tile([P, BATCH, PACK, POS], BF16)
             for t in range(PACK):
                 nc.vector.tensor_scalar_mul(
@@ -120,16 +121,34 @@ def tile_gnn_pb_v_kernel(
                     in0=g_tiles[n][:, :, t, :],
                     scalar1=bn_scale[:, kind, t : t + 1],
                 )
+            return scaled
+
+        def mask_node(n, scaled):
+            masked = work.tile([P, BATCH, PACK, POS], BF16)
+            nc.vector.scalar_tensor_tensor(
+                out=masked[:].rearrange("p b t s -> p (b t s)"),
+                in0=z_tiles[n][:].rearrange("p b t s -> p (b t s)"),
+                scalar=0.0,
+                in1=scaled[:].rearrange("p b t s -> p (b t s)"),
+                op0=ALU.is_gt,
+                op1=ALU.mult,
+            )
+            return masked
+
+        def interleave_node(masked):
             dz = work.tile([P, BATCH, POS, PACK], BF16, align_bytes=64)
-            for b in range(BATCH):
-                nc.vector.scalar_tensor_tensor(
-                    out=dz[:, b],
-                    in0=z_tiles[n][:, b].rearrange("p t s -> p s t"),
-                    scalar=0.0,
-                    in1=scaled[:, b].rearrange("p t s -> p s t"),
-                    op0=ALU.is_gt,
-                    op1=ALU.mult,
-                )
+            nc.vector.tensor_copy(
+                out=dz[:, SCALAR_BATCHES:],
+                in_=masked[:, SCALAR_BATCHES:].rearrange("p b t s -> p b s t"),
+            )
+            nc.scalar.copy(
+                out=dz[:, :SCALAR_BATCHES],
+                in_=masked[:, :SCALAR_BATCHES].rearrange("p b t s -> p b s t"),
+            )
+            return dz
+
+        def finish_node(n, dz):
+            kind = min(n, kinds - 1)
             dz_codes = work.tile([P, COLS], U32, align_bytes=64)
             dz_scales = work.tile([P, COLS], U8, align_bytes=64)
             nc.vector.quantize_mx(
@@ -137,7 +156,6 @@ def tile_gnn_pb_v_kernel(
                 scales=dz_scales[:],
                 in_=dz[:].rearrange("p b s t -> p (b s t)"),
             )
-
             res = results.tile([P, BATCH, OUT_TILES, POS], F32)
             for m in range(OUT_TILES):
                 m_cols = slice(m * P, (m + 1) * P)
@@ -158,3 +176,18 @@ def tile_gnn_pb_v_kernel(
                 out=out[n].rearrange("b (q m) i j -> q b (m i j)", m=OUT_TILES),
                 in_=res[:].rearrange("q b m s -> q b (m s)"),
             )
+
+        scaled_next = scale_node(0)
+        quantize_weight(0)
+        dz_before = None
+        for n in range(NODES):
+            masked = mask_node(n, scaled_next)
+            if n + 1 < NODES:
+                scaled_next = scale_node(n + 1)
+            dz = interleave_node(masked)
+            if n == 0:
+                quantize_weight(1)
+            else:
+                finish_node(n - 1, dz_before)
+            dz_before = dz
+        finish_node(NODES - 1, dz_before)

@@ -26,6 +26,7 @@ BN_SLOTS = 4
 GAMMA_SLOT = 0
 VAR_SLOT = 1
 SCALAR_BATCHES = 3
+DMA_ALIGN = 256
 
 FLOPS = 2 * NODES * COLS * CH * CH
 BYTES = NODES * COLS * CH * (4 + 2 + 4) + 2 * CH * CH * 2 + 2 * 2 * CH * 2
@@ -61,19 +62,19 @@ def tile_gnn_pb_v_kernel(
         z_tiles = []
         for n in range(NODES):
             if n < kinds:
-                w_raw = wpool.tile([P, PACK, CH], BF16)
+                w_raw = wpool.tile([P, PACK, CH], BF16, align_bytes=DMA_ALIGN)
                 nc.sync.dma_start(
                     out=w_raw[:],
                     in_=weights[n][:, CH : 2 * CH].rearrange("(p t) c -> p t c", t=PACK),
                 )
                 w_raws.append(w_raw)
-            g_sb = loads.tile([P, BATCH, PACK, POS], BF16)
+            g_sb = loads.tile([P, BATCH, PACK, POS], BF16, align_bytes=DMA_ALIGN)
             nc.sync.dma_start(
                 out=g_sb[:].rearrange("p b t s -> p b (t s)"),
                 in_=grad_out[n].rearrange("b (p t) i j -> p b (t i j)", t=PACK),
             )
             g_tiles.append(g_sb)
-            z_sb = loads.tile([P, BATCH, PACK, POS], F32)
+            z_sb = loads.tile([P, BATCH, PACK, POS], F32, align_bytes=DMA_ALIGN)
             nc.sync.dma_start(
                 out=z_sb[:].rearrange("p b t s -> p b (t s)"),
                 in_=z[n].rearrange("b (p t) i j -> p b (t i j)", t=PACK),
@@ -156,7 +157,7 @@ def tile_gnn_pb_v_kernel(
                 scales=dz_scales[:],
                 in_=dz[:].rearrange("p b s t -> p (b s t)"),
             )
-            res = results.tile([P, BATCH, OUT_TILES, POS], F32)
+            res = results.tile([P, BATCH, OUT_TILES, POS], F32, align_bytes=DMA_ALIGN)
             for m in range(OUT_TILES):
                 m_cols = slice(m * P, (m + 1) * P)
                 acc = psum.tile([P, COLS], F32)

@@ -148,8 +148,7 @@ def tile_gnn_pb_v_kernel(
             )
             return dz
 
-        def finish_node(n, dz):
-            kind = min(n, kinds - 1)
+        def quantize_node(dz):
             dz_codes = work.tile([P, COLS], U32, align_bytes=64)
             dz_scales = work.tile([P, COLS], U8, align_bytes=64)
             nc.vector.quantize_mx(
@@ -157,6 +156,10 @@ def tile_gnn_pb_v_kernel(
                 scales=dz_scales[:],
                 in_=dz[:].rearrange("p b s t -> p (b s t)"),
             )
+            return dz_codes, dz_scales
+
+        def multiply_node(n, dz_codes, dz_scales):
+            kind = min(n, kinds - 1)
             res = results.tile([P, BATCH, OUT_TILES, POS], F32, align_bytes=DMA_ALIGN)
             for m in range(OUT_TILES):
                 m_cols = slice(m * P, (m + 1) * P)
@@ -170,16 +173,14 @@ def tile_gnn_pb_v_kernel(
                     start=True,
                     stop=True,
                 )
-                nc.scalar.copy(
-                    out=res[:, :, m, :], in_=acc[:].rearrange("p (b s) -> p b s", b=BATCH)
-                )
+                copy_out = nc.vector.tensor_copy if n >= NODES - 2 and m % 2 == 1 else nc.scalar.copy
+                copy_out(out=res[:, :, m, :], in_=acc[:].rearrange("p (b s) -> p b s", b=BATCH))
             nc.sync.dma_start(
                 out=out[n].rearrange("b (q m) i j -> q b (m i j)", m=OUT_TILES),
                 in_=res[:].rearrange("q b m s -> q b (m s)"),
             )
 
         scaled_next = scale_node(0)
-        quantize_weight(0)
         dz_before = None
         for n in range(NODES):
             masked = mask_node(n, scaled_next)
@@ -187,8 +188,12 @@ def tile_gnn_pb_v_kernel(
                 scaled_next = scale_node(n + 1)
             dz = interleave_node(masked)
             if n == 0:
+                quantize_weight(0)
                 quantize_weight(1)
-            else:
-                finish_node(n - 1, dz_before)
-            dz_before = dz
-        finish_node(NODES - 1, dz_before)
+            elif n + 1 < NODES:
+                multiply_node(n - 1, *quantize_node(dz_before))
+            dz_before_that, dz_before = dz_before, dz
+        operands_before = quantize_node(dz_before_that)
+        operands_last = quantize_node(dz_before)
+        multiply_node(NODES - 2, *operands_before)
+        multiply_node(NODES - 1, *operands_last)

@@ -26,7 +26,7 @@ BN_SLOTS = 4
 GAMMA_SLOT = 0
 VAR_SLOT = 1
 SCALAR_BATCHES = 3
-DMA_ALIGN = 256
+DMA_ALIGN = 4096
 
 FLOPS = 2 * NODES * COLS * CH * CH
 BYTES = NODES * COLS * CH * (4 + 2 + 4) + 2 * CH * CH * 2 + 2 * 2 * CH * 2

@@ -26,6 +26,7 @@ BN_SLOTS = 4
 GAMMA_SLOT = 0
 VAR_SLOT = 1
 SCALAR_BATCHES = 3
+RUN = 4
 DMA_ALIGN = 4096
 
 FLOPS = 2 * NODES * COLS * CH * CH
@@ -94,8 +95,8 @@ def tile_gnn_pb_v_kernel(
         for kind in range(kinds):
             w_grouped = wpool.tile([P, OUT_TILES, P, PACK], BF16, align_bytes=64)
             nc.scalar.copy(
-                out=w_grouped[:],
-                in_=w_raws[kind][:].rearrange("p t (q m) -> p m q t", m=OUT_TILES),
+                out=w_grouped[:].rearrange("p m q t -> p q t m"),
+                in_=w_raws[kind][:].rearrange("p t (q m) -> p q t m", m=OUT_TILES),
             )
             w_grouped_tiles.append(w_grouped)
 
@@ -139,12 +140,12 @@ def tile_gnn_pb_v_kernel(
         def interleave_node(masked):
             dz = work.tile([P, BATCH, POS, PACK], BF16, align_bytes=64)
             nc.vector.tensor_copy(
-                out=dz[:, SCALAR_BATCHES:],
-                in_=masked[:, SCALAR_BATCHES:].rearrange("p b t s -> p b s t"),
+                out=dz[:, SCALAR_BATCHES:].rearrange("p b (c i) t -> p b c t i", i=RUN),
+                in_=masked[:, SCALAR_BATCHES:].rearrange("p b t (c i) -> p b c t i", i=RUN),
             )
             nc.scalar.copy(
-                out=dz[:, :SCALAR_BATCHES],
-                in_=masked[:, :SCALAR_BATCHES].rearrange("p b t s -> p b s t"),
+                out=dz[:, :SCALAR_BATCHES].rearrange("p b (c i) t -> p b c t i", i=RUN),
+                in_=masked[:, :SCALAR_BATCHES].rearrange("p b t (c i) -> p b c t i", i=RUN),
             )
             return dz
 

@@ -26,6 +26,7 @@ BN_SLOTS = 4
 GAMMA_SLOT = 0
 VAR_SLOT = 1
 SCALAR_BATCHES = 3
+SCALAR_BATCHES_LAST = 0
 RUN = 4
 DMA_ALIGN = 4096
 
@@ -137,16 +138,18 @@ def tile_gnn_pb_v_kernel(
             )
             return masked
 
-        def interleave_node(masked):
+        def interleave_node(n, masked):
+            scalar_batches = SCALAR_BATCHES if n < NODES - 1 else SCALAR_BATCHES_LAST
             dz = work.tile([P, BATCH, POS, PACK], BF16, align_bytes=64)
             nc.vector.tensor_copy(
-                out=dz[:, SCALAR_BATCHES:].rearrange("p b (c i) t -> p b c t i", i=RUN),
-                in_=masked[:, SCALAR_BATCHES:].rearrange("p b t (c i) -> p b c t i", i=RUN),
+                out=dz[:, scalar_batches:].rearrange("p b (c i) t -> p b c t i", i=RUN),
+                in_=masked[:, scalar_batches:].rearrange("p b t (c i) -> p b c t i", i=RUN),
             )
-            nc.scalar.copy(
-                out=dz[:, :SCALAR_BATCHES].rearrange("p b (c i) t -> p b c t i", i=RUN),
-                in_=masked[:, :SCALAR_BATCHES].rearrange("p b t (c i) -> p b c t i", i=RUN),
-            )
+            if scalar_batches:
+                nc.scalar.copy(
+                    out=dz[:, :scalar_batches].rearrange("p b (c i) t -> p b c t i", i=RUN),
+                    in_=masked[:, :scalar_batches].rearrange("p b t (c i) -> p b c t i", i=RUN),
+                )
             return dz
 
         def quantize_node(dz):
@@ -187,7 +190,7 @@ def tile_gnn_pb_v_kernel(
             masked = mask_node(n, scaled_next)
             if n + 1 < NODES:
                 scaled_next = scale_node(n + 1)
-            dz = interleave_node(masked)
+            dz = interleave_node(n, masked)
             if n == 0:
                 quantize_weight(0)
                 quantize_weight(1)

from contextlib import ExitStack

import concourse.mybir as mybir

F32 = mybir.dt.float32
BF16 = mybir.dt.bfloat16
U32 = mybir.dt.uint32
U8 = mybir.dt.uint8
E4M3_X4 = mybir.dt.float8_e4m3fn_x4
E5M2_X4 = mybir.dt.float8_e5m2_x4
ALU = mybir.AluOpType

P = 128
PACK = 4
NODES = 7
BATCH = 4
CH = 512
POS = 128
COLS = BATCH * POS
OUT_TILES = CH // P
EPS = 1e-5
BN_ROWS = 4
GAMMA_ROW = 0
VAR_ROW = 3
BN_SLOTS = 4
GAMMA_SLOT = 0
VAR_SLOT = 1
SCALAR_BATCHES = 3
SCALAR_BATCHES_LAST = 0
RUN = 4
DMA_ALIGN = 4096

FLOPS = 2 * NODES * COLS * CH * CH
BYTES = NODES * COLS * CH * (4 + 2 + 4) + 2 * CH * CH * 2 + 2 * 2 * CH * 2


def tile_gnn_pb_v_kernel(
    tc, p_nodes, h_nodes, W_decomp_half, bn_decomp_half, W_bg_p, bn_bg_p, z, grad_out, out
):
    nc = tc.nc
    weights = [W_bg_p, W_decomp_half]
    norms = [bn_bg_p, bn_decomp_half]
    kinds = len(weights)

    with ExitStack() as ctx:
        consts = ctx.enter_context(tc.tile_pool(name="consts", bufs=1))
        wpool = ctx.enter_context(tc.tile_pool(name="wpool", bufs=kinds))
        loads = ctx.enter_context(tc.tile_pool(name="loads", bufs=NODES))
        work = ctx.enter_context(tc.tile_pool(name="work", bufs=3))
        results = ctx.enter_context(tc.tile_pool(name="results", bufs=NODES))
        psum = ctx.enter_context(tc.psum_pool(name="psum", bufs=2 * OUT_TILES))
        ctx.enter_context(tc.manual_schedule())

        bn_sb = consts.tile([P, kinds, BN_SLOTS, PACK], BF16)
        for kind in range(kinds):
            table = norms[kind].rearrange("r (p t) -> p r t", t=PACK)
            nc.scalar.dma_start(
                out=bn_sb[:, kind, GAMMA_SLOT : VAR_SLOT + 1, :],
                in_=table[:, GAMMA_ROW : BN_ROWS : VAR_ROW - GAMMA_ROW, :],
            )

        w_raws = []
        g_tiles = []
        z_tiles = []
        for n in range(NODES):
            if n < kinds:
                w_raw = wpool.tile([P, PACK, CH], BF16, align_bytes=DMA_ALIGN)
                nc.sync.dma_start(
                    out=w_raw[:],
                    in_=weights[n][:, CH : 2 * CH].rearrange("(p t) c -> p t c", t=PACK),
                )
                w_raws.append(w_raw)
            g_sb = loads.tile([P, BATCH, PACK, POS], BF16, align_bytes=DMA_ALIGN)
            nc.sync.dma_start(
                out=g_sb[:].rearrange("p b t s -> p b (t s)"),
                in_=grad_out[n].rearrange("b (p t) i j -> p b (t i j)", t=PACK),
            )
            g_tiles.append(g_sb)
            z_sb = loads.tile([P, BATCH, PACK, POS], F32, align_bytes=DMA_ALIGN)
            nc.sync.dma_start(
                out=z_sb[:].rearrange("p b t s -> p b (t s)"),
                in_=z[n].rearrange("b (p t) i j -> p b (t i j)", t=PACK),
            )
            z_tiles.append(z_sb)

        var_eps = consts.tile([P, kinds, PACK], F32)
        nc.vector.tensor_scalar_add(out=var_eps[:], in0=bn_sb[:, :, VAR_SLOT, :], scalar1=EPS)
        std = consts.tile([P, kinds, PACK], F32)
        nc.scalar.sqrt(out=std[:], in_=var_eps[:])
        inv_std = consts.tile([P, kinds, PACK], F32)
        nc.vector.reciprocal(out=inv_std[:], in_=std[:])
        bn_scale = consts.tile([P, kinds, PACK], F32)
        nc.vector.tensor_mul(out=bn_scale[:], in0=inv_std[:], in1=bn_sb[:, :, GAMMA_SLOT, :])

        w_grouped_tiles = []
        for kind in range(kinds):
            w_grouped = wpool.tile([P, OUT_TILES, P, PACK], BF16, align_bytes=64)
            nc.scalar.copy(
                out=w_grouped[:].rearrange("p m q t -> p q t m"),
                in_=w_raws[kind][:].rearrange("p t (q m) -> p q t m", m=OUT_TILES),
            )
            w_grouped_tiles.append(w_grouped)

        w_codes_tiles = []
        w_scales_tiles = []

        def quantize_weight(kind):
            w_codes = wpool.tile([P, CH], U32, align_bytes=64)
            w_scales = wpool.tile([P, CH], U8, align_bytes=64)
            nc.vector.quantize_mx(
                out=w_codes[:].bitcast(E4M3_X4),
                scales=w_scales[:],
                in_=w_grouped_tiles[kind][:].rearrange("p m q t -> p (m q t)"),
            )
            w_codes_tiles.append(w_codes)
            w_scales_tiles.append(w_scales)

        def scale_node(n):
            kind = min(n, kinds - 1)
            scaled = work.tile([P, BATCH, PACK, POS], BF16)
            for t in range(PACK):
                nc.vector.tensor_scalar_mul(
                    out=scaled[:, :, t, :],
                    in0=g_tiles[n][:, :, t, :],
                    scalar1=bn_scale[:, kind, t : t + 1],
                )
            return scaled

        def mask_node(n, scaled):
            masked = work.tile([P, BATCH, PACK, POS], BF16)
            nc.vector.scalar_tensor_tensor(
                out=masked[:].rearrange("p b t s -> p (b t s)"),
                in0=z_tiles[n][:].rearrange("p b t s -> p (b t s)"),
                scalar=0.0,
                in1=scaled[:].rearrange("p b t s -> p (b t s)"),
                op0=ALU.is_gt,
                op1=ALU.mult,
            )
            return masked

        def interleave_node(n, masked):
            scalar_batches = SCALAR_BATCHES if n < NODES - 1 else SCALAR_BATCHES_LAST
            dz = work.tile([P, BATCH, POS, PACK], BF16, align_bytes=64)
            nc.vector.tensor_copy(
                out=dz[:, scalar_batches:].rearrange("p b (c i) t -> p b c t i", i=RUN),
                in_=masked[:, scalar_batches:].rearrange("p b t (c i) -> p b c t i", i=RUN),
            )
            if scalar_batches:
                nc.scalar.copy(
                    out=dz[:, :scalar_batches].rearrange("p b (c i) t -> p b c t i", i=RUN),
                    in_=masked[:, :scalar_batches].rearrange("p b t (c i) -> p b c t i", i=RUN),
                )
            return dz

        def quantize_node(dz):
            dz_codes = work.tile([P, COLS], U32, align_bytes=64)
            dz_scales = work.tile([P, COLS], U8, align_bytes=64)
            nc.vector.quantize_mx(
                out=dz_codes[:].bitcast(E5M2_X4),
                scales=dz_scales[:],
                in_=dz[:].rearrange("p b s t -> p (b s t)"),
            )
            return dz_codes, dz_scales

        def multiply_node(n, dz_codes, dz_scales):
            kind = min(n, kinds - 1)
            res = results.tile([P, BATCH, OUT_TILES, POS], F32, align_bytes=DMA_ALIGN)
            for m in range(OUT_TILES):
                m_cols = slice(m * P, (m + 1) * P)
                acc = psum.tile([P, COLS], F32)
                nc.tensor.matmul_mx(
                    out=acc[:],
                    lhsT=w_codes_tiles[kind][:, m_cols].bitcast(E4M3_X4),
                    lhsT_scale=w_scales_tiles[kind][:, m_cols],
                    rhs=dz_codes[:].bitcast(E5M2_X4),
                    rhs_scale=dz_scales[:],
                    start=True,
                    stop=True,
                )
                copy_out = nc.vector.tensor_copy if n >= NODES - 2 and m % 2 == 1 else nc.scalar.copy
                copy_out(out=res[:, :, m, :], in_=acc[:].rearrange("p (b s) -> p b s", b=BATCH))
            nc.sync.dma_start(
                out=out[n].rearrange("b (q m) i j -> q b (m i j)", m=OUT_TILES),
                in_=res[:].rearrange("q b m s -> q b (m s)"),
            )

        scaled_next = scale_node(0)
        dz_before = None
        for n in range(NODES):
            masked = mask_node(n, scaled_next)
            if n + 1 < NODES:
                scaled_next = scale_node(n + 1)
            dz = interleave_node(n, masked)
            if n == 0:
                quantize_weight(0)
                quantize_weight(1)
            elif n + 1 < NODES:
                multiply_node(n - 1, *quantize_node(dz_before))
            dz_before_that, dz_before = dz_before, dz
        operands_before = quantize_node(dz_before_that)
        operands_last = quantize_node(dz_before)
        multiply_node(NODES - 2, *operands_before)
        multiply_node(NODES - 1, *operands_last)
